import numpy as np
import ml_dtypes


def mxq(x, axis, fmt="e4m3"):
    dtype, down = {"e4m3": (ml_dtypes.float8_e4m3fn, 7), "e5m2": (ml_dtypes.float8_e5m2, 14)}[fmt]
    v = np.moveaxis(np.asarray(x, np.float32).astype(ml_dtypes.bfloat16).astype(np.float64), axis, -1)
    blocks = v.reshape(v.shape[:-1] + (-1, 32))
    amax = np.abs(blocks).max(-1, keepdims=True)
    byte = np.maximum(np.where(amax > 0, np.frexp(amax)[1] - 1 + 127, 0) - down, 1)
    scale = np.exp2(byte - 127.0)
    codes = (blocks / scale).astype(np.float32).astype(dtype).astype(np.float64)
    return np.moveaxis((codes * scale).reshape(v.shape), -1, axis)


WIDE = False


def mx_kscale(k):
    if not WIDE:
        return np.ones(k)
    levels = np.array([10, -10, 5, -5, 0])
    a = np.random.permutation(np.resize(levels, k // 512 * 4)).reshape(k // 512, 4)
    idx = np.arange(k)
    return np.exp2(a[idx // 512, idx % 128 // 32])


BF16 = ml_dtypes.bfloat16


def bf(x):
    return np.asarray(x, np.float32).astype(BF16)


def f64(x):
    return np.asarray(x).astype(np.float64)


B, S, E, HID, H = 2, 512, 2048, 2048, 16
DH = HID // H


def setup_inputs():
    t = mx_kscale(HID)
    kv_rms = np.hypot(6.0 * np.sqrt(S), 0.19 * S)
    return {"q_feat": bf(1.0 + 2.8 * np.random.standard_normal((B, H, S, DH))),
            "kv": bf(np.random.standard_normal((B, H, DH, DH)) * kv_rms * t.reshape(H, 1, DH)),
            "denom": bf(S * DH * (1.0 + 0.1 * np.random.standard_normal((B, H, 1, 1)))),
            "Wo": bf(np.random.standard_normal((HID, E)) * 4.0 / np.sqrt(HID) / t[:, None]),
            "bo": bf(np.random.standard_normal(E) * 0.1)}


def reference(q_feat, kv, denom, Wo, bo):
    qkv = f64(q_feat) @ f64(kv)
    ctx = qkv / f64(denom)
    ctx = ctx.transpose(0, 2, 1, 3).reshape(B, S, HID)
    return (mxq(ctx, 2, "e4m3") @ mxq(f64(Wo), 0, "e4m3")) + f64(bo)

@@ -1,0 +1,167 @@
+from contextlib import ExitStack
+
+import concourse.mybir as mybir
+from concourse.masks import make_identity
+
+BF16 = mybir.dt.bfloat16
+F32 = mybir.dt.float32
+U32 = mybir.dt.uint32
+U8 = mybir.dt.uint8
+FP8X4 = mybir.dt.float8_e4m3fn_x4
+
+B, H, S, DH = 2, 16, 512, 128
+HID = H * DH
+E = 2048
+
+P = 128
+PACK = 4
+PASSES = HID // (P * PACK)
+ROW_TILES = S // P
+N_TILE = 512
+N_CHUNKS = E // N_TILE
+HEAD_GROUPS = B * PASSES
+WO_UNITS = N_CHUNKS * PASSES
+WO_UNITS_EARLY = 2 * PASSES
+
+FLOPS = 2 * B * H * S * DH * DH + 2 * B * S * HID * E
+
+
+def tile_linearattention_pb_kernel(tc, q_feat, kv, denom, Wo, bo, out):
+    nc = tc.nc
+    with ExitStack() as stack:
+        keep = stack.enter_context(tc.tile_pool(name="keep", bufs=1))
+        qt_pool = stack.enter_context(tc.tile_pool(name="qt", bufs=3))
+        ctx_pool = stack.enter_context(tc.tile_pool(name="ctx", bufs=3))
+        wo_pool = stack.enter_context(tc.tile_pool(name="wo", bufs=3))
+        res_pool = stack.enter_context(tc.tile_pool(name="res", bufs=6))
+        psum_a = stack.enter_context(tc.psum_pool(name="psum_a", bufs=4))
+        psum_b = stack.enter_context(tc.psum_pool(name="psum_b", bufs=4))
+
+        den_bf = keep.tile([P, B * H], BF16, name="den_bf")
+        nc.scalar.dma_start(
+            out=den_bf[:], in_=denom.rearrange("b h x y -> (b h x y)").partition_broadcast(P)
+        )
+        ident = keep.tile([P, P], BF16, name="ident")
+        make_identity(nc, ident[:])
+
+        wo_rows = Wo.rearrange("(g t p) n -> g p t n", t=PACK, p=P)
+        bias_sb = keep.tile([P, E], BF16, name="bias_sb")
+        q_sb = []
+        kv_sb = []
+        wo_raw = []
+
+        def load_wo_unit(w):
+            j, g = divmod(w, PASSES)
+            raw = keep.tile([P, PACK, N_TILE], BF16, name="wo_raw%d" % w)
+            nc.sync.dma_start(out=raw[:], in_=wo_rows[g, :, :, j * N_TILE : (j + 1) * N_TILE])
+            wo_raw.append(raw)
+
+        for u in range(HEAD_GROUPS):
+            b, g = divmod(u, PASSES)
+            heads = slice(PACK * g, PACK * (g + 1))
+            q_u = keep.tile([P, PACK, S], BF16, name="q_sb%d" % u)
+            nc.sync.dma_start(
+                out=q_u[:], in_=q_feat[b, heads].rearrange("t (p i) d -> p t (i d)", i=ROW_TILES)
+            )
+            q_sb.append(q_u)
+            kv_u = keep.tile([P, PACK, DH], BF16, name="kv_sb%d" % u)
+            nc.sync.dma_start(out=kv_u[:], in_=kv[b, heads].rearrange("t d e -> d t e"))
+            kv_sb.append(kv_u)
+            load_wo_unit(u)
+        nc.sync.dma_start(out=bias_sb[:], in_=bo.partition_broadcast(P))
+        for w in range(HEAD_GROUPS, WO_UNITS):
+            load_wo_unit(w)
+
+        rden = keep.tile([P, B * H], F32, name="rden")
+        nc.vector.reciprocal(out=rden[:], in_=den_bf[:])
+
+        ctx_codes = keep.tile([P, HEAD_GROUPS, S], U32, name="ctx_codes", align_bytes=64)
+        ctx_scales = keep.tile([P, HEAD_GROUPS, S], U8, name="ctx_scales", align_bytes=64)
+        wo_codes = keep.tile([P, WO_UNITS, N_TILE], U32, name="wo_codes", align_bytes=64)
+        wo_scales = keep.tile([P, WO_UNITS, N_TILE], U8, name="wo_scales", align_bytes=64)
+
+        def transpose_queries(u):
+            qT = qt_pool.tile([P, PACK, S], BF16, name="qT")
+            for t in range(PACK):
+                qT_ps = psum_a.tile([P, S], BF16, name="qT_ps", tag="a")
+                for i in range(ROW_TILES):
+                    rows = slice(i * P, (i + 1) * P)
+                    nc.tensor.transpose(qT_ps[:, rows], q_sb[u][:, t, rows], ident[:])
+                nc.scalar.copy(out=qT[:, t, :], in_=qT_ps[:])
+            return qT
+
+        def make_ctx(u, qT):
+            grouped = ctx_pool.tile([P, S, PACK], BF16, name="ctx_grouped", align_bytes=64)
+            for i in range(ROW_TILES):
+                rows = slice(i * P, (i + 1) * P)
+                ctx_ps = psum_b.tile([P, PACK, P], F32, name="ctx_ps", tag="b")
+                for t in range(PACK):
+                    nc.tensor.matmul(
+                        ctx_ps[:, t, :], lhsT=kv_sb[u][:, t, :], rhs=qT[:, t, rows],
+                        start=True, stop=True,
+                    )
+                nc.vector.tensor_tensor(
+                    out=grouped[:, rows, :],
+                    in0=ctx_ps[:].rearrange("p t s -> p s t"),
+                    in1=rden[:, PACK * u : PACK * (u + 1)].unsqueeze(1).to_broadcast([P, P, PACK]),
+                    op=mybir.AluOpType.mult,
+                )
+            nc.vector.quantize_mx(
+                out=ctx_codes[:, u, :].bitcast(FP8X4),
+                scales=ctx_scales[:, u, :],
+                in_=grouped[:].rearrange("p s t -> p (s t)"),
+            )
+
+        def quantise_wo_unit(w):
+            grouped = wo_pool.tile([P, N_TILE, PACK], BF16, name="wo_grouped", align_bytes=64)
+            nc.scalar.copy(
+                out=grouped[:].rearrange("p (c r) t -> p c t r", r=4),
+                in_=wo_raw[w][:].rearrange("p t (c r) -> p c t r", r=4),
+            )
+            nc.vector.quantize_mx(
+                out=wo_codes[:, w, :].bitcast(FP8X4),
+                scales=wo_scales[:, w, :],
+                in_=grouped[:].rearrange("p n t -> p (n t)"),
+            )
+
+        def project(b, j):
+            cols = slice(j * N_TILE, (j + 1) * N_TILE)
+            psum, tag = (psum_a, "a") if b == 0 else (psum_b, "b")
+            sums = [psum.tile([P, N_TILE], F32, name="sums", tag=tag) for i in range(ROW_TILES)]
+            for g in range(PASSES):
+                u = b * PASSES + g
+                w = j * PASSES + g
+                for i in range(ROW_TILES):
+                    rows = slice(i * P, (i + 1) * P)
+                    nc.tensor.matmul_mx(
+                        out=sums[i][:],
+                        lhsT=ctx_codes[:, u, rows].bitcast(FP8X4),
+                        lhsT_scale=ctx_scales[:, u, rows],
+                        rhs=wo_codes[:, w, :].bitcast(FP8X4),
+                        rhs_scale=wo_scales[:, w, :],
+                        start=(g == 0),
+                        stop=(g == PASSES - 1),
+                    )
+            out_rows = out[b].rearrange("(p i) n -> p i n", i=ROW_TILES)
+            for i in range(ROW_TILES):
+                res = res_pool.tile([P, N_TILE], F32, name="res")
+                nc.vector.tensor_tensor(
+                    out=res[:], in0=sums[i][:], in1=bias_sb[:, cols], op=mybir.AluOpType.add
+                )
+                nc.sync.dma_start(out=out_rows[:, i, cols], in_=res[:])
+
+        qT_next = transpose_queries(0)
+        for u in range(HEAD_GROUPS):
+            qT = qT_next
+            if u + 1 < HEAD_GROUPS:
+                qT_next = transpose_queries(u + 1)
+            make_ctx(u, qT)
+            quantise_wo_unit(u)
+
+        w_next = WO_UNITS_EARLY
+        for j in range(N_CHUNKS):
+            for b in range(B):
+                for w in range(w_next, min(w_next + PASSES // B, WO_UNITS)):
+                    quantise_wo_unit(w)
+                w_next = min(w_next + PASSES // B, WO_UNITS)
+                project(b, j)

@@ -21,7 +21,7 @@ N_TILE = 512
 N_CHUNKS = E // N_TILE
 HEAD_GROUPS = B * PASSES
 WO_UNITS = N_CHUNKS * PASSES
-WO_UNITS_EARLY = 2 * PASSES
+WO_UNITS_EARLY = PASSES
 
 FLOPS = 2 * B * H * S * DH * DH + 2 * B * S * HID * E
 
@@ -29,10 +29,11 @@ FLOPS = 2 * B * H * S * DH * DH + 2 * B * S * HID * E
 def tile_linearattention_pb_kernel(tc, q_feat, kv, denom, Wo, bo, out):
     nc = tc.nc
     with ExitStack() as stack:
+        stack.enter_context(tc.manual_schedule())
         keep = stack.enter_context(tc.tile_pool(name="keep", bufs=1))
+        early_pool = stack.enter_context(tc.tile_pool(name="early", bufs=HEAD_GROUPS))
         qt_pool = stack.enter_context(tc.tile_pool(name="qt", bufs=3))
-        ctx_pool = stack.enter_context(tc.tile_pool(name="ctx", bufs=3))
-        wo_pool = stack.enter_context(tc.tile_pool(name="wo", bufs=3))
+        wo_pool = stack.enter_context(tc.tile_pool(name="wo", bufs=WO_UNITS_EARLY + 2))
         res_pool = stack.enter_context(tc.tile_pool(name="res", bufs=6))
         psum_a = stack.enter_context(tc.psum_pool(name="psum_a", bufs=4))
         psum_b = stack.enter_context(tc.psum_pool(name="psum_b", bufs=4))
@@ -52,14 +53,17 @@ def tile_linearattention_pb_kernel(tc, q_feat, kv, denom, Wo, bo, out):
 
         def load_wo_unit(w):
             j, g = divmod(w, PASSES)
-            raw = keep.tile([P, PACK, N_TILE], BF16, name="wo_raw%d" % w)
+            if w < WO_UNITS // 2:
+                raw = keep.tile([P, PACK, N_TILE], BF16, name="wo_raw%d" % w)
+            else:
+                raw = early_pool.tile([P, PACK, N_TILE], BF16, name="wo_raw", tag="early")
             nc.sync.dma_start(out=raw[:], in_=wo_rows[g, :, :, j * N_TILE : (j + 1) * N_TILE])
             wo_raw.append(raw)
 
         for u in range(HEAD_GROUPS):
             b, g = divmod(u, PASSES)
             heads = slice(PACK * g, PACK * (g + 1))
-            q_u = keep.tile([P, PACK, S], BF16, name="q_sb%d" % u)
+            q_u = early_pool.tile([P, PACK, S], BF16, name="q_sb", tag="early")
             nc.sync.dma_start(
                 out=q_u[:], in_=q_feat[b, heads].rearrange("t (p i) d -> p t (i d)", i=ROW_TILES)
             )
@@ -67,10 +71,12 @@ def tile_linearattention_pb_kernel(tc, q_feat, kv, denom, Wo, bo, out):
             kv_u = keep.tile([P, PACK, DH], BF16, name="kv_sb%d" % u)
             nc.sync.dma_start(out=kv_u[:], in_=kv[b, heads].rearrange("t d e -> d t e"))
             kv_sb.append(kv_u)
-            load_wo_unit(u)
-        nc.sync.dma_start(out=bias_sb[:], in_=bo.partition_broadcast(P))
-        for w in range(HEAD_GROUPS, WO_UNITS):
+            if 1 <= u <= WO_UNITS_EARLY:
+                load_wo_unit(u - 1)
+        for w in range(WO_UNITS_EARLY, WO_UNITS // 2):
             load_wo_unit(w)
+            if w == WO_UNITS_EARLY + PASSES // 2 - 1:
+                nc.sync.dma_start(out=bias_sb[:], in_=bo.partition_broadcast(P))
 
         rden = keep.tile([P, B * H], F32, name="rden")
         nc.vector.reciprocal(out=rden[:], in_=den_bf[:])
@@ -90,8 +96,12 @@ def tile_linearattention_pb_kernel(tc, q_feat, kv, denom, Wo, bo, out):
                 nc.scalar.copy(out=qT[:, t, :], in_=qT_ps[:])
             return qT
 
+        ctx_grouped = []
+        wo_grouped = []
+
         def make_ctx(u, qT):
-            grouped = ctx_pool.tile([P, S, PACK], BF16, name="ctx_grouped", align_bytes=64)
+            grouped = keep.tile([P, S, PACK], BF16, name="ctx_grouped%d" % u, align_bytes=64)
+            ctx_grouped.append(grouped)
             for i in range(ROW_TILES):
                 rows = slice(i * P, (i + 1) * P)
                 ctx_ps = psum_b.tile([P, PACK, P], F32, name="ctx_ps", tag="b")
@@ -106,26 +116,30 @@ def tile_linearattention_pb_kernel(tc, q_feat, kv, denom, Wo, bo, out):
                     in1=rden[:, PACK * u : PACK * (u + 1)].unsqueeze(1).to_broadcast([P, P, PACK]),
                     op=mybir.AluOpType.mult,
                 )
+
+        def quantise_ctx(u):
             nc.vector.quantize_mx(
                 out=ctx_codes[:, u, :].bitcast(FP8X4),
                 scales=ctx_scales[:, u, :],
-                in_=grouped[:].rearrange("p s t -> p (s t)"),
+                in_=ctx_grouped[u][:].rearrange("p s t -> p (s t)"),
             )
 
-        def quantise_wo_unit(w):
+        def regroup_wo_unit(w):
             grouped = wo_pool.tile([P, N_TILE, PACK], BF16, name="wo_grouped", align_bytes=64)
+            wo_grouped.append(grouped)
             nc.scalar.copy(
                 out=grouped[:].rearrange("p (c r) t -> p c t r", r=4),
                 in_=wo_raw[w][:].rearrange("p t (c r) -> p c t r", r=4),
             )
+
+        def quantise_wo_unit(w):
             nc.vector.quantize_mx(
                 out=wo_codes[:, w, :].bitcast(FP8X4),
                 scales=wo_scales[:, w, :],
-                in_=grouped[:].rearrange("p n t -> p (n t)"),
+                in_=wo_grouped[w][:].rearrange("p n t -> p (n t)"),
             )
 
         def project(b, j):
-            cols = slice(j * N_TILE, (j + 1) * N_TILE)
             psum, tag = (psum_a, "a") if b == 0 else (psum_b, "b")
             sums = [psum.tile([P, N_TILE], F32, name="sums", tag=tag) for i in range(ROW_TILES)]
             for g in range(PASSES):
@@ -142,6 +156,10 @@ def tile_linearattention_pb_kernel(tc, q_feat, kv, denom, Wo, bo, out):
                         start=(g == 0),
                         stop=(g == PASSES - 1),
                     )
+            return sums
+
+        def add_bias_and_store(b, j, sums):
+            cols = slice(j * N_TILE, (j + 1) * N_TILE)
             out_rows = out[b].rearrange("(p i) n -> p i n", i=ROW_TILES)
             for i in range(ROW_TILES):
                 res = res_pool.tile([P, N_TILE], F32, name="res")
@@ -156,12 +174,23 @@ def tile_linearattention_pb_kernel(tc, q_feat, kv, denom, Wo, bo, out):
             if u + 1 < HEAD_GROUPS:
                 qT_next = transpose_queries(u + 1)
             make_ctx(u, qT)
-            quantise_wo_unit(u)
+            if u < WO_UNITS_EARLY:
+                regroup_wo_unit(u)
+        for w in range(WO_UNITS // 2, WO_UNITS):
+            load_wo_unit(w)
+
+        for g in range(PASSES):
+            quantise_ctx(g)
+            quantise_wo_unit(g)
+        for g in range(PASSES):
+            quantise_ctx(PASSES + g)
 
         w_next = WO_UNITS_EARLY
         for j in range(N_CHUNKS):
             for b in range(B):
+                sums = project(b, j)
                 for w in range(w_next, min(w_next + PASSES // B, WO_UNITS)):
+                    regroup_wo_unit(w)
                     quantise_wo_unit(w)
                 w_next = min(w_next + PASSES // B, WO_UNITS)
-                project(b, j)
+                add_bias_and_store(b, j, sums)

@@ -34,7 +34,7 @@ def tile_linearattention_pb_kernel(tc, q_feat, kv, denom, Wo, bo, out):
         early_pool = stack.enter_context(tc.tile_pool(name="early", bufs=HEAD_GROUPS))
         qt_pool = stack.enter_context(tc.tile_pool(name="qt", bufs=3))
         wo_pool = stack.enter_context(tc.tile_pool(name="wo", bufs=WO_UNITS_EARLY + 2))
-        res_pool = stack.enter_context(tc.tile_pool(name="res", bufs=6))
+        res_pool = stack.enter_context(tc.tile_pool(name="res", bufs=10))
         psum_a = stack.enter_context(tc.psum_pool(name="psum_a", bufs=4))
         psum_b = stack.enter_context(tc.psum_pool(name="psum_b", bufs=4))
 
@@ -166,7 +166,7 @@ def tile_linearattention_pb_kernel(tc, q_feat, kv, denom, Wo, bo, out):
                 nc.vector.tensor_tensor(
                     out=res[:], in0=sums[i][:], in1=bias_sb[:, cols], op=mybir.AluOpType.add
                 )
-                nc.sync.dma_start(out=out_rows[:, i, cols], in_=res[:])
+                nc.gpsimd.dma_start(out=out_rows[:, i, cols], in_=res[:])
 
         qT_next = transpose_queries(0)
         for u in range(HEAD_GROUPS):

@@ -33,8 +33,8 @@ def tile_linearattention_pb_kernel(tc, q_feat, kv, denom, Wo, bo, out):
         keep = stack.enter_context(tc.tile_pool(name="keep", bufs=1))
         early_pool = stack.enter_context(tc.tile_pool(name="early", bufs=HEAD_GROUPS))
         qt_pool = stack.enter_context(tc.tile_pool(name="qt", bufs=3))
-        wo_pool = stack.enter_context(tc.tile_pool(name="wo", bufs=WO_UNITS_EARLY + 2))
-        res_pool = stack.enter_context(tc.tile_pool(name="res", bufs=10))
+        wo_pool = stack.enter_context(tc.tile_pool(name="wo", bufs=WO_UNITS_EARLY + 1))
+        late_pool = stack.enter_context(tc.tile_pool(name="late", bufs=HEAD_GROUPS + 4))
         psum_a = stack.enter_context(tc.psum_pool(name="psum_a", bufs=4))
         psum_b = stack.enter_context(tc.psum_pool(name="psum_b", bufs=4))
 
@@ -45,8 +45,14 @@ def tile_linearattention_pb_kernel(tc, q_feat, kv, denom, Wo, bo, out):
         ident = keep.tile([P, P], BF16, name="ident")
         make_identity(nc, ident[:])
 
+        bias_row = keep.tile([P, E], BF16, name="bias_row")
+        nc.vector.memset(bias_row[:], 0.0)
+        nc.scalar.dma_start(out=bias_row[0:1, :], in_=bo.rearrange("(o n) -> o n", o=1))
+        ones = keep.tile([P, P], BF16, name="ones")
+        nc.vector.memset(ones[:], 1.0)
+        bias_sb = keep.tile([P, E], F32, name="bias_sb")
+
         wo_rows = Wo.rearrange("(g t p) n -> g p t n", t=PACK, p=P)
-        bias_sb = keep.tile([P, E], BF16, name="bias_sb")
         q_sb = []
         kv_sb = []
         wo_raw = []
@@ -75,8 +81,6 @@ def tile_linearattention_pb_kernel(tc, q_feat, kv, denom, Wo, bo, out):
                 load_wo_unit(u - 1)
         for w in range(WO_UNITS_EARLY, WO_UNITS // 2):
             load_wo_unit(w)
-            if w == WO_UNITS_EARLY + PASSES // 2 - 1:
-                nc.sync.dma_start(out=bias_sb[:], in_=bo.partition_broadcast(P))
 
         rden = keep.tile([P, B * H], F32, name="rden")
         nc.vector.reciprocal(out=rden[:], in_=den_bf[:])
@@ -100,7 +104,7 @@ def tile_linearattention_pb_kernel(tc, q_feat, kv, denom, Wo, bo, out):
         wo_grouped = []
 
         def make_ctx(u, qT):
-            grouped = keep.tile([P, S, PACK], BF16, name="ctx_grouped%d" % u, align_bytes=64)
+            grouped = late_pool.tile([P, S, PACK], BF16, name="ctx_grouped", tag="late", align_bytes=64)
             ctx_grouped.append(grouped)
             for i in range(ROW_TILES):
                 rows = slice(i * P, (i + 1) * P)
@@ -116,6 +120,13 @@ def tile_linearattention_pb_kernel(tc, q_feat, kv, denom, Wo, bo, out):
                     in1=rden[:, PACK * u : PACK * (u + 1)].unsqueeze(1).to_broadcast([P, P, PACK]),
                     op=mybir.AluOpType.mult,
                 )
+
+        def broadcast_bias():
+            for j in range(N_CHUNKS):
+                cols = slice(j * N_TILE, (j + 1) * N_TILE)
+                bias_ps = psum_a.tile([P, N_TILE], F32, name="bias_ps", tag="a")
+                nc.tensor.matmul(bias_ps[:], lhsT=ones[:], rhs=bias_row[:, cols], start=True, stop=True)
+                nc.scalar.copy(out=bias_sb[:, cols], in_=bias_ps[:])
 
         def quantise_ctx(u):
             nc.vector.quantize_mx(
@@ -140,39 +151,46 @@ def tile_linearattention_pb_kernel(tc, q_feat, kv, denom, Wo, bo, out):
             )
 
         def project(b, j):
-            psum, tag = (psum_a, "a") if b == 0 else (psum_b, "b")
+            psum, tag = (psum_b, "b") if b == 0 else (psum_a, "a")
             sums = [psum.tile([P, N_TILE], F32, name="sums", tag=tag) for i in range(ROW_TILES)]
-            for g in range(PASSES):
+            if j == 0:
+                order = [(g, i) for g in range(PASSES) for i in range(ROW_TILES)]
+            else:
+                order = [(g, i) for i in range(ROW_TILES) for g in range(PASSES)]
+            for g, i in order:
                 u = b * PASSES + g
                 w = j * PASSES + g
-                for i in range(ROW_TILES):
-                    rows = slice(i * P, (i + 1) * P)
-                    nc.tensor.matmul_mx(
-                        out=sums[i][:],
-                        lhsT=ctx_codes[:, u, rows].bitcast(FP8X4),
-                        lhsT_scale=ctx_scales[:, u, rows],
-                        rhs=wo_codes[:, w, :].bitcast(FP8X4),
-                        rhs_scale=wo_scales[:, w, :],
-                        start=(g == 0),
-                        stop=(g == PASSES - 1),
-                    )
+                rows = slice(i * P, (i + 1) * P)
+                nc.tensor.matmul_mx(
+                    out=sums[i][:],
+                    lhsT=ctx_codes[:, u, rows].bitcast(FP8X4),
+                    lhsT_scale=ctx_scales[:, u, rows],
+                    rhs=wo_codes[:, w, :].bitcast(FP8X4),
+                    rhs_scale=wo_scales[:, w, :],
+                    start=(g == 0),
+                    stop=(g == PASSES - 1),
+                )
             return sums
 
         def add_bias_and_store(b, j, sums):
             cols = slice(j * N_TILE, (j + 1) * N_TILE)
             out_rows = out[b].rearrange("(p i) n -> p i n", i=ROW_TILES)
-            for i in range(ROW_TILES):
-                res = res_pool.tile([P, N_TILE], F32, name="res")
-                nc.vector.tensor_tensor(
-                    out=res[:], in0=sums[i][:], in1=bias_sb[:, cols], op=mybir.AluOpType.add
-                )
-                nc.gpsimd.dma_start(out=out_rows[:, i, cols], in_=res[:])
+            for i0 in range(0, ROW_TILES, 2):
+                res = late_pool.tile([P, 2, N_TILE], F32, name="res", tag="late", align_bytes=64)
+                for i in (i0, i0 + 1):
+                    nc.vector.tensor_tensor(
+                        out=res[:, i - i0, :], in0=sums[i][:], in1=bias_sb[:, cols],
+                        op=mybir.AluOpType.add,
+                    )
+                nc.sync.dma_start(out=out_rows[:, i0 : i0 + 2, cols], in_=res[:])
 
         qT_next = transpose_queries(0)
         for u in range(HEAD_GROUPS):
             qT = qT_next
             if u + 1 < HEAD_GROUPS:
                 qT_next = transpose_queries(u + 1)
+            else:
+                broadcast_bias()
             make_ctx(u, qT)
             if u < WO_UNITS_EARLY:
                 regroup_wo_unit(u)

@@ -21,7 +21,6 @@ N_TILE = 512
 N_CHUNKS = E // N_TILE
 HEAD_GROUPS = B * PASSES
 WO_UNITS = N_CHUNKS * PASSES
-WO_UNITS_EARLY = PASSES
 
 FLOPS = 2 * B * H * S * DH * DH + 2 * B * S * HID * E
 
@@ -33,7 +32,7 @@ def tile_linearattention_pb_kernel(tc, q_feat, kv, denom, Wo, bo, out):
         keep = stack.enter_context(tc.tile_pool(name="keep", bufs=1))
         early_pool = stack.enter_context(tc.tile_pool(name="early", bufs=HEAD_GROUPS))
         qt_pool = stack.enter_context(tc.tile_pool(name="qt", bufs=3))
-        wo_pool = stack.enter_context(tc.tile_pool(name="wo", bufs=WO_UNITS_EARLY + 1))
+        wo_pool = stack.enter_context(tc.tile_pool(name="wo", bufs=PASSES + 1))
         late_pool = stack.enter_context(tc.tile_pool(name="late", bufs=HEAD_GROUPS + 4))
         psum_a = stack.enter_context(tc.psum_pool(name="psum_a", bufs=4))
         psum_b = stack.enter_context(tc.psum_pool(name="psum_b", bufs=4))
@@ -42,30 +41,19 @@ def tile_linearattention_pb_kernel(tc, q_feat, kv, denom, Wo, bo, out):
         nc.scalar.dma_start(
             out=den_bf[:], in_=denom.rearrange("b h x y -> (b h x y)").partition_broadcast(P)
         )
-        ident = keep.tile([P, P], BF16, name="ident")
-        make_identity(nc, ident[:])
-
         bias_row = keep.tile([P, E], BF16, name="bias_row")
         nc.vector.memset(bias_row[:], 0.0)
         nc.scalar.dma_start(out=bias_row[0:1, :], in_=bo.rearrange("(o n) -> o n", o=1))
         ones = keep.tile([P, P], BF16, name="ones")
         nc.vector.memset(ones[:], 1.0)
         bias_sb = keep.tile([P, E], F32, name="bias_sb")
+        ident = keep.tile([P, P], BF16, name="ident")
+        make_identity(nc, ident[:])
+        rden = keep.tile([P, B * H], F32, name="rden")
+        nc.vector.reciprocal(out=rden[:], in_=den_bf[:])
 
-        wo_rows = Wo.rearrange("(g t p) n -> g p t n", t=PACK, p=P)
         q_sb = []
         kv_sb = []
-        wo_raw = []
-
-        def load_wo_unit(w):
-            j, g = divmod(w, PASSES)
-            if w < WO_UNITS // 2:
-                raw = keep.tile([P, PACK, N_TILE], BF16, name="wo_raw%d" % w)
-            else:
-                raw = early_pool.tile([P, PACK, N_TILE], BF16, name="wo_raw", tag="early")
-            nc.sync.dma_start(out=raw[:], in_=wo_rows[g, :, :, j * N_TILE : (j + 1) * N_TILE])
-            wo_raw.append(raw)
-
         for u in range(HEAD_GROUPS):
             b, g = divmod(u, PASSES)
             heads = slice(PACK * g, PACK * (g + 1))
@@ -77,56 +65,57 @@ def tile_linearattention_pb_kernel(tc, q_feat, kv, denom, Wo, bo, out):
             kv_u = keep.tile([P, PACK, DH], BF16, name="kv_sb%d" % u)
             nc.sync.dma_start(out=kv_u[:], in_=kv[b, heads].rearrange("t d e -> d t e"))
             kv_sb.append(kv_u)
-            if 1 <= u <= WO_UNITS_EARLY:
-                load_wo_unit(u - 1)
-        for w in range(WO_UNITS_EARLY, WO_UNITS // 2):
-            load_wo_unit(w)
 
-        rden = keep.tile([P, B * H], F32, name="rden")
-        nc.vector.reciprocal(out=rden[:], in_=den_bf[:])
+        wo_rows = Wo.rearrange("(g t p) n -> g p t n", t=PACK, p=P)
+        wo_raw = []
+
+        def load_wo_unit(w):
+            j, g = divmod(w, PASSES)
+            if w < WO_UNITS // 2:
+                raw = keep.tile([P, PACK, N_TILE], BF16, name="wo_raw%d" % w)
+            else:
+                raw = early_pool.tile([P, PACK, N_TILE], BF16, name="wo_raw", tag="early")
+            nc.sync.dma_start(out=raw[:], in_=wo_rows[g, :, :, j * N_TILE : (j + 1) * N_TILE])
+            wo_raw.append(raw)
+
+        for w in range(WO_UNITS // 2):
+            load_wo_unit(w)
 
         ctx_codes = keep.tile([P, HEAD_GROUPS, S], U32, name="ctx_codes", align_bytes=64)
         ctx_scales = keep.tile([P, HEAD_GROUPS, S], U8, name="ctx_scales", align_bytes=64)
         wo_codes = keep.tile([P, WO_UNITS, N_TILE], U32, name="wo_codes", align_bytes=64)
         wo_scales = keep.tile([P, WO_UNITS, N_TILE], U8, name="wo_scales", align_bytes=64)
-
-        def transpose_queries(u):
-            qT = qt_pool.tile([P, PACK, S], BF16, name="qT")
-            for t in range(PACK):
-                qT_ps = psum_a.tile([P, S], BF16, name="qT_ps", tag="a")
-                for i in range(ROW_TILES):
-                    rows = slice(i * P, (i + 1) * P)
-                    nc.tensor.transpose(qT_ps[:, rows], q_sb[u][:, t, rows], ident[:])
-                nc.scalar.copy(out=qT[:, t, :], in_=qT_ps[:])
-            return qT
-
         ctx_grouped = []
         wo_grouped = []
 
-        def make_ctx(u, qT):
+        def make_ctx(u):
+            qT = qt_pool.tile([P, ROW_TILES, PACK, P], BF16, name="qT")
+            for i in range(ROW_TILES):
+                qT_ps = psum_a.tile([P, PACK, P], BF16, name="qT_ps", tag="a")
+                for t in range(PACK):
+                    nc.tensor.transpose(qT_ps[:, t, :], q_sb[u][:, t, i * P : (i + 1) * P], ident[:])
+                nc.scalar.copy(out=qT[:, i, :, :], in_=qT_ps[:])
             grouped = late_pool.tile([P, S, PACK], BF16, name="ctx_grouped", tag="late", align_bytes=64)
             ctx_grouped.append(grouped)
             for i in range(ROW_TILES):
-                rows = slice(i * P, (i + 1) * P)
                 ctx_ps = psum_b.tile([P, PACK, P], F32, name="ctx_ps", tag="b")
                 for t in range(PACK):
                     nc.tensor.matmul(
-                        ctx_ps[:, t, :], lhsT=kv_sb[u][:, t, :], rhs=qT[:, t, rows],
+                        ctx_ps[:, t, :], lhsT=kv_sb[u][:, t, :], rhs=qT[:, i, t, :],
                         start=True, stop=True,
                     )
                 nc.vector.tensor_tensor(
-                    out=grouped[:, rows, :],
+                    out=grouped[:, i * P : (i + 1) * P, :],
                     in0=ctx_ps[:].rearrange("p t s -> p s t"),
                     in1=rden[:, PACK * u : PACK * (u + 1)].unsqueeze(1).to_broadcast([P, P, PACK]),
                     op=mybir.AluOpType.mult,
                 )
 
-        def broadcast_bias():
-            for j in range(N_CHUNKS):
-                cols = slice(j * N_TILE, (j + 1) * N_TILE)
-                bias_ps = psum_a.tile([P, N_TILE], F32, name="bias_ps", tag="a")
-                nc.tensor.matmul(bias_ps[:], lhsT=ones[:], rhs=bias_row[:, cols], start=True, stop=True)
-                nc.scalar.copy(out=bias_sb[:, cols], in_=bias_ps[:])
+        def broadcast_bias(j):
+            cols = slice(j * N_TILE, (j + 1) * N_TILE)
+            bias_ps = psum_a.tile([P, N_TILE], F32, name="bias_ps", tag="a")
+            nc.tensor.matmul(bias_ps[:], lhsT=ones[:], rhs=bias_row[:, cols], start=True, stop=True)
+            nc.scalar.copy(out=bias_sb[:, cols], in_=bias_ps[:])
 
         def quantise_ctx(u):
             nc.vector.quantize_mx(
@@ -153,7 +142,7 @@ def tile_linearattention_pb_kernel(tc, q_feat, kv, denom, Wo, bo, out):
         def project(b, j):
             psum, tag = (psum_b, "b") if b == 0 else (psum_a, "a")
             sums = [psum.tile([P, N_TILE], F32, name="sums", tag=tag) for i in range(ROW_TILES)]
-            if j == 0:
+            if (j, b) != (N_CHUNKS - 1, B - 1):
                 order = [(g, i) for g in range(PASSES) for i in range(ROW_TILES)]
             else:
                 order = [(g, i) for i in range(ROW_TILES) for g in range(PASSES)]
@@ -172,43 +161,40 @@ def tile_linearattention_pb_kernel(tc, q_feat, kv, denom, Wo, bo, out):
                 )
             return sums
 
-        def add_bias_and_store(b, j, sums):
+        def add_bias_and_store(b, j, sums, i0):
             cols = slice(j * N_TILE, (j + 1) * N_TILE)
+            res = late_pool.tile([P, 2, N_TILE], F32, name="res", tag="late", align_bytes=64)
+            for i in (i0, i0 + 1):
+                nc.vector.tensor_tensor(
+                    out=res[:, i - i0, :], in0=sums[i][:], in1=bias_sb[:, cols],
+                    op=mybir.AluOpType.add,
+                )
             out_rows = out[b].rearrange("(p i) n -> p i n", i=ROW_TILES)
-            for i0 in range(0, ROW_TILES, 2):
-                res = late_pool.tile([P, 2, N_TILE], F32, name="res", tag="late", align_bytes=64)
-                for i in (i0, i0 + 1):
-                    nc.vector.tensor_tensor(
-                        out=res[:, i - i0, :], in0=sums[i][:], in1=bias_sb[:, cols],
-                        op=mybir.AluOpType.add,
-                    )
-                nc.sync.dma_start(out=out_rows[:, i0 : i0 + 2, cols], in_=res[:])
+            nc.sync.dma_start(out=out_rows[:, i0 : i0 + 2, cols], in_=res[:])
 
-        qT_next = transpose_queries(0)
         for u in range(HEAD_GROUPS):
-            qT = qT_next
-            if u + 1 < HEAD_GROUPS:
-                qT_next = transpose_queries(u + 1)
-            else:
-                broadcast_bias()
-            make_ctx(u, qT)
-            if u < WO_UNITS_EARLY:
-                regroup_wo_unit(u)
+            make_ctx(u)
+            if u < N_CHUNKS:
+                broadcast_bias(u)
         for w in range(WO_UNITS // 2, WO_UNITS):
             load_wo_unit(w)
 
+        for w in range(PASSES):
+            regroup_wo_unit(w)
         for g in range(PASSES):
             quantise_ctx(g)
             quantise_wo_unit(g)
         for g in range(PASSES):
             quantise_ctx(PASSES + g)
 
-        w_next = WO_UNITS_EARLY
         for j in range(N_CHUNKS):
             for b in range(B):
                 sums = project(b, j)
-                for w in range(w_next, min(w_next + PASSES // B, WO_UNITS)):
+                w_first = (j + 1) * PASSES + b * (PASSES // B)
+                ahead = [w for w in (w_first, w_first + 1) if w < WO_UNITS]
+                for w in ahead:
                     regroup_wo_unit(w)
-                    quantise_wo_unit(w)
-                w_next = min(w_next + PASSES // B, WO_UNITS)
-                add_bias_and_store(b, j, sums)
+                for half in range(2):
+                    if ahead:
+                        quantise_wo_unit(ahead[half])
+                    add_bias_and_store(b, j, sums, 2 * half)

@@ -21,6 +21,9 @@ N_TILE = 512
 N_CHUNKS = E // N_TILE
 HEAD_GROUPS = B * PASSES
 WO_UNITS = N_CHUNKS * PASSES
+STEPS = HEAD_GROUPS * ROW_TILES
+AHEAD = 2
+GPSIMD_PIECES = 4
 
 FLOPS = 2 * B * H * S * DH * DH + 2 * B * S * HID * E
 
@@ -31,8 +34,8 @@ def tile_linearattention_pb_kernel(tc, q_feat, kv, denom, Wo, bo, out):
         stack.enter_context(tc.manual_schedule())
         keep = stack.enter_context(tc.tile_pool(name="keep", bufs=1))
         early_pool = stack.enter_context(tc.tile_pool(name="early", bufs=HEAD_GROUPS))
-        qt_pool = stack.enter_context(tc.tile_pool(name="qt", bufs=3))
-        wo_pool = stack.enter_context(tc.tile_pool(name="wo", bufs=PASSES + 1))
+        qt_pool = stack.enter_context(tc.tile_pool(name="qt", bufs=AHEAD + 3))
+        wo_pool = stack.enter_context(tc.tile_pool(name="wo", bufs=PASSES + 2))
         late_pool = stack.enter_context(tc.tile_pool(name="late", bufs=HEAD_GROUPS + 4))
         psum_a = stack.enter_context(tc.psum_pool(name="psum_a", bufs=4))
         psum_b = stack.enter_context(tc.psum_pool(name="psum_b", bufs=4))
@@ -88,28 +91,35 @@ def tile_linearattention_pb_kernel(tc, q_feat, kv, denom, Wo, bo, out):
         ctx_grouped = []
         wo_grouped = []
 
-        def make_ctx(u):
-            qT = qt_pool.tile([P, ROW_TILES, PACK, P], BF16, name="qT")
-            for i in range(ROW_TILES):
-                qT_ps = psum_a.tile([P, PACK, P], BF16, name="qT_ps", tag="a")
-                for t in range(PACK):
-                    nc.tensor.transpose(qT_ps[:, t, :], q_sb[u][:, t, i * P : (i + 1) * P], ident[:])
-                nc.scalar.copy(out=qT[:, i, :, :], in_=qT_ps[:])
-            grouped = late_pool.tile([P, S, PACK], BF16, name="ctx_grouped", tag="late", align_bytes=64)
-            ctx_grouped.append(grouped)
-            for i in range(ROW_TILES):
-                ctx_ps = psum_b.tile([P, PACK, P], F32, name="ctx_ps", tag="b")
-                for t in range(PACK):
-                    nc.tensor.matmul(
-                        ctx_ps[:, t, :], lhsT=kv_sb[u][:, t, :], rhs=qT[:, i, t, :],
-                        start=True, stop=True,
-                    )
-                nc.vector.tensor_tensor(
-                    out=grouped[:, i * P : (i + 1) * P, :],
-                    in0=ctx_ps[:].rearrange("p t s -> p s t"),
-                    in1=rden[:, PACK * u : PACK * (u + 1)].unsqueeze(1).to_broadcast([P, P, PACK]),
-                    op=mybir.AluOpType.mult,
+        qT_tiles = []
+
+        def transpose_step(k):
+            u, i = divmod(k, ROW_TILES)
+            qT_ps = psum_a.tile([P, PACK, P], BF16, name="qT_ps", tag="a")
+            for t in range(PACK):
+                nc.tensor.transpose(qT_ps[:, t, :], q_sb[u][:, t, i * P : (i + 1) * P], ident[:])
+            qT = qt_pool.tile([P, PACK, P], BF16, name="qT")
+            nc.scalar.copy(out=qT[:], in_=qT_ps[:])
+            qT_tiles.append(qT)
+
+        def ctx_step(k):
+            u, i = divmod(k, ROW_TILES)
+            if i == 0:
+                ctx_grouped.append(
+                    late_pool.tile([P, S, PACK], BF16, name="ctx_grouped", tag="late", align_bytes=64)
                 )
+            ctx_ps = psum_b.tile([P, PACK, P], F32, name="ctx_ps", tag="b")
+            for t in range(PACK):
+                nc.tensor.matmul(
+                    ctx_ps[:, t, :], lhsT=kv_sb[u][:, t, :], rhs=qT_tiles[k][:, t, :],
+                    start=True, stop=True,
+                )
+            nc.vector.tensor_tensor(
+                out=ctx_grouped[u][:, i * P : (i + 1) * P, :],
+                in0=ctx_ps[:].rearrange("p t s -> p s t"),
+                in1=rden[:, PACK * u : PACK * (u + 1)].unsqueeze(1).to_broadcast([P, P, PACK]),
+                op=mybir.AluOpType.mult,
+            )
 
         def broadcast_bias(j):
             cols = slice(j * N_TILE, (j + 1) * N_TILE)
@@ -127,10 +137,23 @@ def tile_linearattention_pb_kernel(tc, q_feat, kv, denom, Wo, bo, out):
         def regroup_wo_unit(w):
             grouped = wo_pool.tile([P, N_TILE, PACK], BF16, name="wo_grouped", align_bytes=64)
             wo_grouped.append(grouped)
-            nc.scalar.copy(
-                out=grouped[:].rearrange("p (c r) t -> p c t r", r=4),
-                in_=wo_raw[w][:].rearrange("p t (c r) -> p c t r", r=4),
-            )
+            if w % PASSES == 0:
+                width = N_TILE // GPSIMD_PIECES
+                for c in range(GPSIMD_PIECES):
+                    cols = slice(c * width, (c + 1) * width)
+                    nc.gpsimd.tensor_scalar(
+                        out=grouped[:, cols, :],
+                        in0=wo_raw[w][:, :, cols].rearrange("p t n -> p n t"),
+                        scalar1=1.0,
+                        scalar2=0.0,
+                        op0=mybir.AluOpType.mult,
+                        op1=mybir.AluOpType.add,
+                    )
+            else:
+                nc.scalar.copy(
+                    out=grouped[:].rearrange("p (c r) t -> p c t r", r=4),
+                    in_=wo_raw[w][:].rearrange("p t (c r) -> p c t r", r=4),
+                )
 
         def quantise_wo_unit(w):
             nc.vector.quantize_mx(
@@ -172,9 +195,14 @@ def tile_linearattention_pb_kernel(tc, q_feat, kv, denom, Wo, bo, out):
             out_rows = out[b].rearrange("(p i) n -> p i n", i=ROW_TILES)
             nc.sync.dma_start(out=out_rows[:, i0 : i0 + 2, cols], in_=res[:])
 
-        for u in range(HEAD_GROUPS):
-            make_ctx(u)
-            if u < N_CHUNKS:
+        for k in range(AHEAD):
+            transpose_step(k)
+        for k in range(STEPS):
+            if k + AHEAD < STEPS:
+                transpose_step(k + AHEAD)
+            ctx_step(k)
+            u, i = divmod(k, ROW_TILES)
+            if i == ROW_TILES - 1 and u < N_CHUNKS:
                 broadcast_bias(u)
         for w in range(WO_UNITS // 2, WO_UNITS):
             load_wo_unit(w)

@@ -23,7 +23,6 @@ HEAD_GROUPS = B * PASSES
 WO_UNITS = N_CHUNKS * PASSES
 STEPS = HEAD_GROUPS * ROW_TILES
 AHEAD = 2
-GPSIMD_PIECES = 4
 
 FLOPS = 2 * B * H * S * DH * DH + 2 * B * S * HID * E
 
@@ -137,23 +136,10 @@ def tile_linearattention_pb_kernel(tc, q_feat, kv, denom, Wo, bo, out):
         def regroup_wo_unit(w):
             grouped = wo_pool.tile([P, N_TILE, PACK], BF16, name="wo_grouped", align_bytes=64)
             wo_grouped.append(grouped)
-            if w % PASSES == 0:
-                width = N_TILE // GPSIMD_PIECES
-                for c in range(GPSIMD_PIECES):
-                    cols = slice(c * width, (c + 1) * width)
-                    nc.gpsimd.tensor_scalar(
-                        out=grouped[:, cols, :],
-                        in0=wo_raw[w][:, :, cols].rearrange("p t n -> p n t"),
-                        scalar1=1.0,
-                        scalar2=0.0,
-                        op0=mybir.AluOpType.mult,
-                        op1=mybir.AluOpType.add,
-                    )
-            else:
-                nc.scalar.copy(
-                    out=grouped[:].rearrange("p (c r) t -> p c t r", r=4),
-                    in_=wo_raw[w][:].rearrange("p t (c r) -> p c t r", r=4),
-                )
+            nc.scalar.copy(
+                out=grouped[:].rearrange("p (c r) t -> p c t r", r=4),
+                in_=wo_raw[w][:].rearrange("p t (c r) -> p c t r", r=4),
+            )
 
         def quantise_wo_unit(w):
             nc.vector.quantize_mx(

from contextlib import ExitStack

import concourse.mybir as mybir
from concourse.masks import make_identity

BF16 = mybir.dt.bfloat16
F32 = mybir.dt.float32
U32 = mybir.dt.uint32
U8 = mybir.dt.uint8
FP8X4 = mybir.dt.float8_e4m3fn_x4

B, H, S, DH = 2, 16, 512, 128
HID = H * DH
E = 2048

P = 128
PACK = 4
PASSES = HID // (P * PACK)
ROW_TILES = S // P
N_TILE = 512
N_CHUNKS = E // N_TILE
HEAD_GROUPS = B * PASSES
WO_UNITS = N_CHUNKS * PASSES
STEPS = HEAD_GROUPS * ROW_TILES
AHEAD = 2

FLOPS = 2 * B * H * S * DH * DH + 2 * B * S * HID * E


def tile_linearattention_pb_kernel(tc, q_feat, kv, denom, Wo, bo, out):
    nc = tc.nc
    with ExitStack() as stack:
        stack.enter_context(tc.manual_schedule())
        keep = stack.enter_context(tc.tile_pool(name="keep", bufs=1))
        early_pool = stack.enter_context(tc.tile_pool(name="early", bufs=HEAD_GROUPS))
        qt_pool = stack.enter_context(tc.tile_pool(name="qt", bufs=AHEAD + 3))
        wo_pool = stack.enter_context(tc.tile_pool(name="wo", bufs=PASSES + 2))
        late_pool = stack.enter_context(tc.tile_pool(name="late", bufs=HEAD_GROUPS + 4))
        psum_a = stack.enter_context(tc.psum_pool(name="psum_a", bufs=4))
        psum_b = stack.enter_context(tc.psum_pool(name="psum_b", bufs=4))

        den_bf = keep.tile([P, B * H], BF16, name="den_bf")
        nc.scalar.dma_start(
            out=den_bf[:], in_=denom.rearrange("b h x y -> (b h x y)").partition_broadcast(P)
        )
        bias_row = keep.tile([P, E], BF16, name="bias_row")
        nc.vector.memset(bias_row[:], 0.0)
        nc.scalar.dma_start(out=bias_row[0:1, :], in_=bo.rearrange("(o n) -> o n", o=1))
        ones = keep.tile([P, P], BF16, name="ones")
        nc.vector.memset(ones[:], 1.0)
        bias_sb = keep.tile([P, E], F32, name="bias_sb")
        ident = keep.tile([P, P], BF16, name="ident")
        make_identity(nc, ident[:])
        rden = keep.tile([P, B * H], F32, name="rden")
        nc.vector.reciprocal(out=rden[:], in_=den_bf[:])

        q_sb = []
        kv_sb = []
        for u in range(HEAD_GROUPS):
            b, g = divmod(u, PASSES)
            heads = slice(PACK * g, PACK * (g + 1))
            q_u = early_pool.tile([P, PACK, S], BF16, name="q_sb", tag="early")
            nc.sync.dma_start(
                out=q_u[:], in_=q_feat[b, heads].rearrange("t (p i) d -> p t (i d)", i=ROW_TILES)
            )
            q_sb.append(q_u)
            kv_u = keep.tile([P, PACK, DH], BF16, name="kv_sb%d" % u)
            nc.sync.dma_start(out=kv_u[:], in_=kv[b, heads].rearrange("t d e -> d t e"))
            kv_sb.append(kv_u)

        wo_rows = Wo.rearrange("(g t p) n -> g p t n", t=PACK, p=P)
        wo_raw = []

        def load_wo_unit(w):
            j, g = divmod(w, PASSES)
            if w < WO_UNITS // 2:
                raw = keep.tile([P, PACK, N_TILE], BF16, name="wo_raw%d" % w)
            else:
                raw = early_pool.tile([P, PACK, N_TILE], BF16, name="wo_raw", tag="early")
            nc.sync.dma_start(out=raw[:], in_=wo_rows[g, :, :, j * N_TILE : (j + 1) * N_TILE])
            wo_raw.append(raw)

        for w in range(WO_UNITS // 2):
            load_wo_unit(w)

        ctx_codes = keep.tile([P, HEAD_GROUPS, S], U32, name="ctx_codes", align_bytes=64)
        ctx_scales = keep.tile([P, HEAD_GROUPS, S], U8, name="ctx_scales", align_bytes=64)
        wo_codes = keep.tile([P, WO_UNITS, N_TILE], U32, name="wo_codes", align_bytes=64)
        wo_scales = keep.tile([P, WO_UNITS, N_TILE], U8, name="wo_scales", align_bytes=64)
        ctx_grouped = []
        wo_grouped = []

        qT_tiles = []

        def transpose_step(k):
            u, i = divmod(k, ROW_TILES)
            qT_ps = psum_a.tile([P, PACK, P], BF16, name="qT_ps", tag="a")
            for t in range(PACK):
                nc.tensor.transpose(qT_ps[:, t, :], q_sb[u][:, t, i * P : (i + 1) * P], ident[:])
            qT = qt_pool.tile([P, PACK, P], BF16, name="qT")
            nc.scalar.copy(out=qT[:], in_=qT_ps[:])
            qT_tiles.append(qT)

        def ctx_step(k):
            u, i = divmod(k, ROW_TILES)
            if i == 0:
                ctx_grouped.append(
                    late_pool.tile([P, S, PACK], BF16, name="ctx_grouped", tag="late", align_bytes=64)
                )
            ctx_ps = psum_b.tile([P, PACK, P], F32, name="ctx_ps", tag="b")
            for t in range(PACK):
                nc.tensor.matmul(
                    ctx_ps[:, t, :], lhsT=kv_sb[u][:, t, :], rhs=qT_tiles[k][:, t, :],
                    start=True, stop=True,
                )
            nc.vector.tensor_tensor(
                out=ctx_grouped[u][:, i * P : (i + 1) * P, :],
                in0=ctx_ps[:].rearrange("p t s -> p s t"),
                in1=rden[:, PACK * u : PACK * (u + 1)].unsqueeze(1).to_broadcast([P, P, PACK]),
                op=mybir.AluOpType.mult,
            )

        def broadcast_bias(j):
            cols = slice(j * N_TILE, (j + 1) * N_TILE)
            bias_ps = psum_a.tile([P, N_TILE], F32, name="bias_ps", tag="a")
            nc.tensor.matmul(bias_ps[:], lhsT=ones[:], rhs=bias_row[:, cols], start=True, stop=True)
            nc.scalar.copy(out=bias_sb[:, cols], in_=bias_ps[:])

        def quantise_ctx(u):
            nc.vector.quantize_mx(
                out=ctx_codes[:, u, :].bitcast(FP8X4),
                scales=ctx_scales[:, u, :],
                in_=ctx_grouped[u][:].rearrange("p s t -> p (s t)"),
            )

        def regroup_wo_unit(w):
            grouped = wo_pool.tile([P, N_TILE, PACK], BF16, name="wo_grouped", align_bytes=64)
            wo_grouped.append(grouped)
            nc.scalar.copy(
                out=grouped[:].rearrange("p (c r) t -> p c t r", r=4),
                in_=wo_raw[w][:].rearrange("p t (c r) -> p c t r", r=4),
            )

        def quantise_wo_unit(w):
            nc.vector.quantize_mx(
                out=wo_codes[:, w, :].bitcast(FP8X4),
                scales=wo_scales[:, w, :],
                in_=wo_grouped[w][:].rearrange("p n t -> p (n t)"),
            )

        def project(b, j):
            psum, tag = (psum_b, "b") if b == 0 else (psum_a, "a")
            sums = [psum.tile([P, N_TILE], F32, name="sums", tag=tag) for i in range(ROW_TILES)]
            if (j, b) != (N_CHUNKS - 1, B - 1):
                order = [(g, i) for g in range(PASSES) for i in range(ROW_TILES)]
            else:
                order = [(g, i) for i in range(ROW_TILES) for g in range(PASSES)]
            for g, i in order:
                u = b * PASSES + g
                w = j * PASSES + g
                rows = slice(i * P, (i + 1) * P)
                nc.tensor.matmul_mx(
                    out=sums[i][:],
                    lhsT=ctx_codes[:, u, rows].bitcast(FP8X4),
                    lhsT_scale=ctx_scales[:, u, rows],
                    rhs=wo_codes[:, w, :].bitcast(FP8X4),
                    rhs_scale=wo_scales[:, w, :],
                    start=(g == 0),
                    stop=(g == PASSES - 1),
                )
            return sums

        def add_bias_and_store(b, j, sums, i0):
            cols = slice(j * N_TILE, (j + 1) * N_TILE)
            res = late_pool.tile([P, 2, N_TILE], F32, name="res", tag="late", align_bytes=64)
            for i in (i0, i0 + 1):
                nc.vector.tensor_tensor(
                    out=res[:, i - i0, :], in0=sums[i][:], in1=bias_sb[:, cols],
                    op=mybir.AluOpType.add,
                )
            out_rows = out[b].rearrange("(p i) n -> p i n", i=ROW_TILES)
            nc.sync.dma_start(out=out_rows[:, i0 : i0 + 2, cols], in_=res[:])

        for k in range(AHEAD):
            transpose_step(k)
        for k in range(STEPS):
            if k + AHEAD < STEPS:
                transpose_step(k + AHEAD)
            ctx_step(k)
            u, i = divmod(k, ROW_TILES)
            if i == ROW_TILES - 1 and u < N_CHUNKS:
                broadcast_bias(u)
        for w in range(WO_UNITS // 2, WO_UNITS):
            load_wo_unit(w)

        for w in range(PASSES):
            regroup_wo_unit(w)
        for g in range(PASSES):
            quantise_ctx(g)
            quantise_wo_unit(g)
        for g in range(PASSES):
            quantise_ctx(PASSES + g)

        for j in range(N_CHUNKS):
            for b in range(B):
                sums = project(b, j)
                w_first = (j + 1) * PASSES + b * (PASSES // B)
                ahead = [w for w in (w_first, w_first + 1) if w < WO_UNITS]
                for w in ahead:
                    regroup_wo_unit(w)
                for half in range(2):
                    if ahead:
                        quantise_wo_unit(ahead[half])
                    add_bias_and_store(b, j, sums, 2 * half)
